import numpy as np
import ml_dtypes


def mxq(x, axis, fmt="e4m3"):
    dtype, down = {"e4m3": (ml_dtypes.float8_e4m3fn, 7), "e5m2": (ml_dtypes.float8_e5m2, 14)}[fmt]
    v = np.moveaxis(np.asarray(x, np.float32).astype(ml_dtypes.bfloat16).astype(np.float64), axis, -1)
    blocks = v.reshape(v.shape[:-1] + (-1, 32))
    amax = np.abs(blocks).max(-1, keepdims=True)
    byte = np.maximum(np.where(amax > 0, np.frexp(amax)[1] - 1 + 127, 0) - down, 1)
    scale = np.exp2(byte - 127.0)
    codes = (blocks / scale).astype(np.float32).astype(dtype).astype(np.float64)
    return np.moveaxis((codes * scale).reshape(v.shape), -1, axis)


WIDE = False


def mx_kscale(k):
    if not WIDE:
        return np.ones(k)
    levels = np.array([20, -20, 10, -10, 0])
    a = np.random.permutation(np.resize(levels, k // 512 * 4)).reshape(k // 512, 4)
    idx = np.arange(k)
    return np.exp2(a[idx // 512, idx % 128 // 32])


BF16 = ml_dtypes.bfloat16


def bf(x):
    return np.asarray(x, np.float32).astype(BF16)


def f64(x):
    return np.asarray(x).astype(np.float64)


M, I, O = 512, 2048, 2048
SPARSITY = 0.98


def _build_mask():
    num_connections = int((1 - SPARSITY) * I * O)
    cpn = max(1, num_connections // O)
    rows = np.arange(O)[:, None]
    cols = (rows * cpn + np.arange(cpn)[None, :]) % I
    mask = np.zeros((O, I))
    mask[np.repeat(np.arange(O), cpn), cols.reshape(-1)] = 1.0
    return mask, cpn


def setup_inputs():
    s = mx_kscale(M)[:, None]
    mask_np, cpn = _build_mask()
    x = np.random.standard_normal((M, I)) * s
    weight = np.random.standard_normal((O, I)) * np.sqrt(2.0 / cpn)
    bias = np.random.standard_normal(O) * 0.1
    g = np.random.standard_normal((M, O)) * np.exp2(np.random.randint(-12, 1, (M, 1))) / s
    return {"x": bf(x), "weight": bf(weight), "bias": bf(bias), "mask": bf(mask_np), "grad_out": bf(g)}


def reference(x, weight, bias, mask, grad_out):
    gw = mxq(f64(grad_out), 0, "e5m2").T @ mxq(f64(x), 0, "e4m3")
    return gw * f64(mask)

@@ -1,0 +1,119 @@
+from contextlib import ExitStack
+
+import concourse.mybir as mybir
+
+BF16 = mybir.dt.bfloat16
+F32 = mybir.dt.float32
+U32 = mybir.dt.uint32
+U8 = mybir.dt.uint8
+E4M3_X4 = mybir.dt.float8_e4m3fn_x4
+E5M2_X4 = mybir.dt.float8_e5m2_x4
+
+P = 128
+PACK = 4
+TOKENS = P * PACK
+IN_F = 2048
+OUT_F = 2048
+N_TILE = 512
+N_TILES = IN_F // N_TILE
+ROWS = 4
+GROUP = P * ROWS
+GROUPS = OUT_F // GROUP
+STORE_ROWS = 2
+RESULT_BUFS = 5
+PSUM_BANKS = 8
+
+FLOPS = 2 * TOKENS * IN_F * OUT_F
+BYTES = 2 * TOKENS * IN_F + 2 * TOKENS * OUT_F + 2 * OUT_F * IN_F + 4 * OUT_F * IN_F
+
+
+def quantise(nc, grouped, codes, scales, cols, fp8_x4):
+    nc.vector.quantize_mx(
+        out=codes[:, cols].bitcast(fp8_x4),
+        scales=scales[:, cols],
+        in_=grouped[:],
+    )
+
+
+def tile_structuredconnection_kernel(tc, x, weight, bias, mask, grad_out, out):
+    nc = tc.nc
+    mask_groups = mask.rearrange("(t m e) i -> t m e i", m=P, e=ROWS)
+    out_groups = out.rearrange("(t m e) i -> t m e i", m=P, e=ROWS)
+
+    with ExitStack() as pools:
+        keep = pools.enter_context(tc.tile_pool(name="keep", bufs=1))
+        stage = pools.enter_context(tc.tile_pool(name="stage", bufs=N_TILES))
+        results = pools.enter_context(tc.tile_pool(name="results", bufs=RESULT_BUFS))
+        psum = pools.enter_context(tc.psum_pool(name="psum", bufs=PSUM_BANKS))
+
+        x_raw = keep.tile([P, PACK, IN_F], BF16)
+        nc.sync.dma_start(out=x_raw[:], in_=x.rearrange("(p j) w -> p j w", j=PACK))
+        g_raw = keep.tile([P, PACK, OUT_F], BF16)
+        nc.sync.dma_start(out=g_raw[:], in_=grad_out.rearrange("(p j) w -> p j w", j=PACK))
+        mask_sb = []
+        for t in range(GROUPS):
+            mask_t = keep.tile([P, ROWS, IN_F], BF16, name="mask%d" % t)
+            nc.sync.dma_start(out=mask_t[:], in_=mask_groups[t])
+            mask_sb.append(mask_t)
+
+        x_codes = keep.tile([P, IN_F], U32, align_bytes=64)
+        x_scales = keep.tile([P, IN_F], U8, align_bytes=64)
+        g_codes = keep.tile([P, OUT_F], U32, align_bytes=64)
+        g_scales = keep.tile([P, OUT_F], U8, align_bytes=64)
+
+        x_cols = [slice(c * N_TILE, (c + 1) * N_TILE) for c in range(N_TILES)]
+        x_grouped = []
+        for c in range(N_TILES):
+            xg = stage.tile([P, N_TILE * PACK], BF16, align_bytes=64)
+            dst = xg[:].rearrange("p (c i j) -> p c j i", i=4, j=PACK)
+            src = x_raw[:, :, x_cols[c]].rearrange("p j (c i) -> p c j i", i=4)
+            if c < N_TILES - 1:
+                nc.vector.tensor_copy(out=dst, in_=src)
+            else:
+                nc.scalar.copy(out=dst, in_=src)
+            x_grouped.append(xg)
+            if c >= 1:
+                quantise(nc, x_grouped[c - 1], x_codes, x_scales, x_cols[c - 1], E4M3_X4)
+        quantise(nc, x_grouped[N_TILES - 1], x_codes, x_scales, x_cols[N_TILES - 1], E4M3_X4)
+
+        g_cols = [slice(t * GROUP, (t + 1) * GROUP) for t in range(GROUPS)]
+        g_grouped = []
+        for t in range(GROUPS):
+            gg = stage.tile([P, GROUP * PACK], BF16, align_bytes=64)
+            dst = gg[:].rearrange("p (e m j) -> p m j e", e=ROWS, j=PACK)
+            src = g_raw[:, :, g_cols[t]].rearrange("p j (m e) -> p m j e", e=ROWS)
+            if t == 0:
+                nc.vector.tensor_copy(out=dst, in_=src)
+            else:
+                nc.scalar.copy(out=dst, in_=src)
+            g_grouped.append(gg)
+        quantise(nc, g_grouped[0], g_codes, g_scales, g_cols[0], E5M2_X4)
+
+        for t in range(GROUPS):
+            if t + 1 < GROUPS:
+                quantise(nc, g_grouped[t + 1], g_codes, g_scales, g_cols[t + 1], E5M2_X4)
+            for first_row in range(0, ROWS, STORE_ROWS):
+                result = results.tile([P, STORE_ROWS, IN_F], F32)
+                for r in range(STORE_ROWS):
+                    e = first_row + r
+                    m_cols = slice((t * ROWS + e) * P, (t * ROWS + e + 1) * P)
+                    for n_cols in x_cols:
+                        acc = psum.tile([P, N_TILE], F32)
+                        nc.tensor.matmul_mx(
+                            out=acc[:],
+                            lhsT=g_codes[:, m_cols].bitcast(E5M2_X4),
+                            lhsT_scale=g_scales[:, m_cols],
+                            rhs=x_codes[:, n_cols].bitcast(E4M3_X4),
+                            rhs_scale=x_scales[:, n_cols],
+                            start=True,
+                            stop=True,
+                        )
+                        nc.vector.tensor_tensor(
+                            out=result[:, r, n_cols],
+                            in0=acc[:],
+                            in1=mask_sb[t][:, e, n_cols],
+                            op=mybir.AluOpType.mult,
+                        )
+                nc.sync.dma_start(
+                    out=out_groups[t][:, first_row : first_row + STORE_ROWS, :], in_=result[:]
+                )

@@ -16,11 +16,13 @@ IN_F = 2048
 OUT_F = 2048
 N_TILE = 512
 N_TILES = IN_F // N_TILE
-ROWS = 4
-GROUP = P * ROWS
-GROUPS = OUT_F // GROUP
-STORE_ROWS = 2
-RESULT_BUFS = 5
+ROWS = OUT_F // P
+CHUNK_ROWS = 4
+CHUNKS = ROWS // CHUNK_ROWS
+MASK_LOADS = (4, 4, 8)
+STORES = (4, 4, 4, 2, 2)
+RESULT_ROWS = 4
+RESULT_BUFS = 3
 PSUM_BANKS = 8
 
 FLOPS = 2 * TOKENS * IN_F * OUT_F
@@ -37,8 +39,8 @@ def quantise(nc, grouped, codes, scales, cols, fp8_x4):
 
 def tile_structuredconnection_kernel(tc, x, weight, bias, mask, grad_out, out):
     nc = tc.nc
-    mask_groups = mask.rearrange("(t m e) i -> t m e i", m=P, e=ROWS)
-    out_groups = out.rearrange("(t m e) i -> t m e i", m=P, e=ROWS)
+    mask_rows = mask.rearrange("(m e) i -> m e i", e=ROWS)
+    out_rows = out.rearrange("(m e) i -> m e i", e=ROWS)
 
     with ExitStack() as pools:
         keep = pools.enter_context(tc.tile_pool(name="keep", bufs=1))
@@ -50,11 +52,12 @@ def tile_structuredconnection_kernel(tc, x, weight, bias, mask, grad_out, out):
         nc.sync.dma_start(out=x_raw[:], in_=x.rearrange("(p j) w -> p j w", j=PACK))
         g_raw = keep.tile([P, PACK, OUT_F], BF16)
         nc.sync.dma_start(out=g_raw[:], in_=grad_out.rearrange("(p j) w -> p j w", j=PACK))
-        mask_sb = []
-        for t in range(GROUPS):
-            mask_t = keep.tile([P, ROWS, IN_F], BF16, name="mask%d" % t)
-            nc.sync.dma_start(out=mask_t[:], in_=mask_groups[t])
-            mask_sb.append(mask_t)
+        mask_of_row = []
+        for rows in MASK_LOADS:
+            e0 = len(mask_of_row)
+            mask_t = keep.tile([P, rows, IN_F], BF16, name="mask%d" % e0)
+            nc.sync.dma_start(out=mask_t[:], in_=mask_rows[:, e0 : e0 + rows, :])
+            mask_of_row.extend([(mask_t, r) for r in range(rows)])
 
         x_codes = keep.tile([P, IN_F], U32, align_bytes=64)
         x_scales = keep.tile([P, IN_F], U8, align_bytes=64)
@@ -64,7 +67,7 @@ def tile_structuredconnection_kernel(tc, x, weight, bias, mask, grad_out, out):
         x_cols = [slice(c * N_TILE, (c + 1) * N_TILE) for c in range(N_TILES)]
         x_grouped = []
         for c in range(N_TILES):
-            xg = stage.tile([P, N_TILE * PACK], BF16, align_bytes=64)
+            xg = stage.tile([P, N_TILE * PACK], BF16, align_bytes=64, name="grouped")
             dst = xg[:].rearrange("p (c i j) -> p c j i", i=4, j=PACK)
             src = x_raw[:, :, x_cols[c]].rearrange("p j (c i) -> p c j i", i=4)
             if c < N_TILES - 1:
@@ -76,12 +79,13 @@ def tile_structuredconnection_kernel(tc, x, weight, bias, mask, grad_out, out):
                 quantise(nc, x_grouped[c - 1], x_codes, x_scales, x_cols[c - 1], E4M3_X4)
         quantise(nc, x_grouped[N_TILES - 1], x_codes, x_scales, x_cols[N_TILES - 1], E4M3_X4)
 
-        g_cols = [slice(t * GROUP, (t + 1) * GROUP) for t in range(GROUPS)]
+        g_cols = [slice(t * N_TILE, (t + 1) * N_TILE) for t in range(CHUNKS)]
+        g_by_row = g_raw[:].rearrange("p j (m e) -> p m j e", e=ROWS)
         g_grouped = []
-        for t in range(GROUPS):
-            gg = stage.tile([P, GROUP * PACK], BF16, align_bytes=64)
-            dst = gg[:].rearrange("p (e m j) -> p m j e", e=ROWS, j=PACK)
-            src = g_raw[:, :, g_cols[t]].rearrange("p j (m e) -> p m j e", e=ROWS)
+        for t in range(CHUNKS):
+            gg = stage.tile([P, N_TILE * PACK], BF16, align_bytes=64, name="grouped")
+            dst = gg[:].rearrange("p (e m j) -> p m j e", e=CHUNK_ROWS, j=PACK)
+            src = g_by_row[:, :, :, t * CHUNK_ROWS : (t + 1) * CHUNK_ROWS]
             if t == 0:
                 nc.vector.tensor_copy(out=dst, in_=src)
             else:
@@ -89,31 +93,31 @@ def tile_structuredconnection_kernel(tc, x, weight, bias, mask, grad_out, out):
             g_grouped.append(gg)
         quantise(nc, g_grouped[0], g_codes, g_scales, g_cols[0], E5M2_X4)
 
-        for t in range(GROUPS):
-            if t + 1 < GROUPS:
-                quantise(nc, g_grouped[t + 1], g_codes, g_scales, g_cols[t + 1], E5M2_X4)
-            for first_row in range(0, ROWS, STORE_ROWS):
-                result = results.tile([P, STORE_ROWS, IN_F], F32)
-                for r in range(STORE_ROWS):
-                    e = first_row + r
-                    m_cols = slice((t * ROWS + e) * P, (t * ROWS + e + 1) * P)
-                    for n_cols in x_cols:
-                        acc = psum.tile([P, N_TILE], F32)
-                        nc.tensor.matmul_mx(
-                            out=acc[:],
-                            lhsT=g_codes[:, m_cols].bitcast(E5M2_X4),
-                            lhsT_scale=g_scales[:, m_cols],
-                            rhs=x_codes[:, n_cols].bitcast(E4M3_X4),
-                            rhs_scale=x_scales[:, n_cols],
-                            start=True,
-                            stop=True,
-                        )
-                        nc.vector.tensor_tensor(
-                            out=result[:, r, n_cols],
-                            in0=acc[:],
-                            in1=mask_sb[t][:, e, n_cols],
-                            op=mybir.AluOpType.mult,
-                        )
-                nc.sync.dma_start(
-                    out=out_groups[t][:, first_row : first_row + STORE_ROWS, :], in_=result[:]
-                )
+        e = 0
+        for rows in STORES:
+            result = results.tile([P, RESULT_ROWS, IN_F], F32)
+            for r in range(rows):
+                if e % CHUNK_ROWS == 0 and e // CHUNK_ROWS + 1 < CHUNKS:
+                    t = e // CHUNK_ROWS + 1
+                    quantise(nc, g_grouped[t], g_codes, g_scales, g_cols[t], E5M2_X4)
+                mask_t, mask_r = mask_of_row[e]
+                m_cols = slice(e * P, (e + 1) * P)
+                for n_cols in x_cols:
+                    acc = psum.tile([P, N_TILE], F32)
+                    nc.tensor.matmul_mx(
+                        out=acc[:],
+                        lhsT=g_codes[:, m_cols].bitcast(E5M2_X4),
+                        lhsT_scale=g_scales[:, m_cols],
+                        rhs=x_codes[:, n_cols].bitcast(E4M3_X4),
+                        rhs_scale=x_scales[:, n_cols],
+                        start=True,
+                        stop=True,
+                    )
+                    nc.vector.tensor_tensor(
+                        out=result[:, r, n_cols],
+                        in0=acc[:],
+                        in1=mask_t[:, mask_r, n_cols],
+                        op=mybir.AluOpType.mult,
+                    )
+                e += 1
+            nc.sync.dma_start(out=out_rows[:, e - rows : e, :], in_=result[:, :rows, :])

@@ -49,7 +49,9 @@ def tile_structuredconnection_kernel(tc, x, weight, bias, mask, grad_out, out):
         psum = pools.enter_context(tc.psum_pool(name="psum", bufs=PSUM_BANKS))
 
         x_raw = keep.tile([P, PACK, IN_F], BF16)
-        nc.sync.dma_start(out=x_raw[:], in_=x.rearrange("(p j) w -> p j w", j=PACK))
+        x_rows = x.rearrange("(p j) w -> p j w", j=PACK)
+        nc.sync.dma_start(out=x_raw[:, :1, :], in_=x_rows[:, :1, :])
+        nc.sync.dma_start(out=x_raw[:, 1:, :], in_=x_rows[:, 1:, :])
         g_raw = keep.tile([P, PACK, OUT_F], BF16)
         nc.sync.dma_start(out=g_raw[:], in_=grad_out.rearrange("(p j) w -> p j w", j=PACK))
         mask_of_row = []

@@ -19,7 +19,11 @@ N_TILES = IN_F // N_TILE
 ROWS = OUT_F // P
 CHUNK_ROWS = 4
 CHUNKS = ROWS // CHUNK_ROWS
-MASK_LOADS = (4, 4, 8)
+LAST_ROW = ROWS - 1
+LAST_COLS = slice(IN_F // 2, IN_F)
+FIRST_COLS = slice(0, IN_F // 2)
+EIGHT_STEP = 4
+EIGHT_SPAN = 8 * EIGHT_STEP
 STORES = (4, 4, 4, 2, 2)
 RESULT_ROWS = 4
 RESULT_BUFS = 3
@@ -48,6 +52,7 @@ def tile_structuredconnection_kernel(tc, x, weight, bias, mask, grad_out, out):
         results = pools.enter_context(tc.tile_pool(name="results", bufs=RESULT_BUFS))
         psum = pools.enter_context(tc.psum_pool(name="psum", bufs=PSUM_BANKS))
 
+        pools.enter_context(tc.manual_schedule(engines={mybir.EngineType.SP}))
         x_raw = keep.tile([P, PACK, IN_F], BF16)
         x_rows = x.rearrange("(p j) w -> p j w", j=PACK)
         nc.sync.dma_start(out=x_raw[:, :1, :], in_=x_rows[:, :1, :])
@@ -55,11 +60,38 @@ def tile_structuredconnection_kernel(tc, x, weight, bias, mask, grad_out, out):
         g_raw = keep.tile([P, PACK, OUT_F], BF16)
         nc.sync.dma_start(out=g_raw[:], in_=grad_out.rearrange("(p j) w -> p j w", j=PACK))
         mask_of_row = []
-        for rows in MASK_LOADS:
+
+        def load_mask(rows):
             e0 = len(mask_of_row)
             mask_t = keep.tile([P, rows, IN_F], BF16, name="mask%d" % e0)
             nc.sync.dma_start(out=mask_t[:], in_=mask_rows[:, e0 : e0 + rows, :])
             mask_of_row.extend([(mask_t, r) for r in range(rows)])
+
+        mask_last = keep.tile([P, 1, IN_F], BF16)
+        eights = []
+        for p0 in range(0, P, EIGHT_SPAN):
+            for r in range(EIGHT_STEP):
+                eights.append(slice(p0 + r, p0 + EIGHT_SPAN, EIGHT_STEP))
+
+        def load_eights(sets):
+            for eight in sets:
+                nc.sync.dma_start(
+                    out=mask_last[eight, 0, LAST_COLS],
+                    in_=mask_rows[eight, LAST_ROW, LAST_COLS],
+                )
+
+        load_mask(4)
+        load_eights(eights[:4])
+        load_mask(4)
+        load_eights(eights[4:8])
+        load_mask(4)
+        load_eights(eights[8:10])
+        nc.sync.dma_start(
+            out=mask_last[:, 0, FIRST_COLS], in_=mask_rows[:, LAST_ROW, FIRST_COLS]
+        )
+        load_mask(3)
+        load_eights(eights[10:])
+        mask_of_row.append((mask_last, 0))
 
         x_codes = keep.tile([P, IN_F], U32, align_bytes=64)
         x_scales = keep.tile([P, IN_F], U8, align_bytes=64)

from contextlib import ExitStack

import concourse.mybir as mybir

BF16 = mybir.dt.bfloat16
F32 = mybir.dt.float32
U32 = mybir.dt.uint32
U8 = mybir.dt.uint8
E4M3_X4 = mybir.dt.float8_e4m3fn_x4
E5M2_X4 = mybir.dt.float8_e5m2_x4

P = 128
PACK = 4
TOKENS = P * PACK
IN_F = 2048
OUT_F = 2048
N_TILE = 512
N_TILES = IN_F // N_TILE
ROWS = OUT_F // P
CHUNK_ROWS = 4
CHUNKS = ROWS // CHUNK_ROWS
LAST_ROW = ROWS - 1
LAST_COLS = slice(IN_F // 2, IN_F)
FIRST_COLS = slice(0, IN_F // 2)
EIGHT_STEP = 4
EIGHT_SPAN = 8 * EIGHT_STEP
STORES = (4, 4, 4, 2, 2)
RESULT_ROWS = 4
RESULT_BUFS = 3
PSUM_BANKS = 8

FLOPS = 2 * TOKENS * IN_F * OUT_F
BYTES = 2 * TOKENS * IN_F + 2 * TOKENS * OUT_F + 2 * OUT_F * IN_F + 4 * OUT_F * IN_F


def quantise(nc, grouped, codes, scales, cols, fp8_x4):
    nc.vector.quantize_mx(
        out=codes[:, cols].bitcast(fp8_x4),
        scales=scales[:, cols],
        in_=grouped[:],
    )


def tile_structuredconnection_kernel(tc, x, weight, bias, mask, grad_out, out):
    nc = tc.nc
    mask_rows = mask.rearrange("(m e) i -> m e i", e=ROWS)
    out_rows = out.rearrange("(m e) i -> m e i", e=ROWS)

    with ExitStack() as pools:
        keep = pools.enter_context(tc.tile_pool(name="keep", bufs=1))
        stage = pools.enter_context(tc.tile_pool(name="stage", bufs=N_TILES))
        results = pools.enter_context(tc.tile_pool(name="results", bufs=RESULT_BUFS))
        psum = pools.enter_context(tc.psum_pool(name="psum", bufs=PSUM_BANKS))

        pools.enter_context(tc.manual_schedule(engines={mybir.EngineType.SP}))
        x_raw = keep.tile([P, PACK, IN_F], BF16)
        x_rows = x.rearrange("(p j) w -> p j w", j=PACK)
        nc.sync.dma_start(out=x_raw[:, :1, :], in_=x_rows[:, :1, :])
        nc.sync.dma_start(out=x_raw[:, 1:, :], in_=x_rows[:, 1:, :])
        g_raw = keep.tile([P, PACK, OUT_F], BF16)
        nc.sync.dma_start(out=g_raw[:], in_=grad_out.rearrange("(p j) w -> p j w", j=PACK))
        mask_of_row = []

        def load_mask(rows):
            e0 = len(mask_of_row)
            mask_t = keep.tile([P, rows, IN_F], BF16, name="mask%d" % e0)
            nc.sync.dma_start(out=mask_t[:], in_=mask_rows[:, e0 : e0 + rows, :])
            mask_of_row.extend([(mask_t, r) for r in range(rows)])

        mask_last = keep.tile([P, 1, IN_F], BF16)
        eights = []
        for p0 in range(0, P, EIGHT_SPAN):
            for r in range(EIGHT_STEP):
                eights.append(slice(p0 + r, p0 + EIGHT_SPAN, EIGHT_STEP))

        def load_eights(sets):
            for eight in sets:
                nc.sync.dma_start(
                    out=mask_last[eight, 0, LAST_COLS],
                    in_=mask_rows[eight, LAST_ROW, LAST_COLS],
                )

        load_mask(4)
        load_eights(eights[:4])
        load_mask(4)
        load_eights(eights[4:8])
        load_mask(4)
        load_eights(eights[8:10])
        nc.sync.dma_start(
            out=mask_last[:, 0, FIRST_COLS], in_=mask_rows[:, LAST_ROW, FIRST_COLS]
        )
        load_mask(3)
        load_eights(eights[10:])
        mask_of_row.append((mask_last, 0))

        x_codes = keep.tile([P, IN_F], U32, align_bytes=64)
        x_scales = keep.tile([P, IN_F], U8, align_bytes=64)
        g_codes = keep.tile([P, OUT_F], U32, align_bytes=64)
        g_scales = keep.tile([P, OUT_F], U8, align_bytes=64)

        x_cols = [slice(c * N_TILE, (c + 1) * N_TILE) for c in range(N_TILES)]
        x_grouped = []
        for c in range(N_TILES):
            xg = stage.tile([P, N_TILE * PACK], BF16, align_bytes=64, name="grouped")
            dst = xg[:].rearrange("p (c i j) -> p c j i", i=4, j=PACK)
            src = x_raw[:, :, x_cols[c]].rearrange("p j (c i) -> p c j i", i=4)
            if c < N_TILES - 1:
                nc.vector.tensor_copy(out=dst, in_=src)
            else:
                nc.scalar.copy(out=dst, in_=src)
            x_grouped.append(xg)
            if c >= 1:
                quantise(nc, x_grouped[c - 1], x_codes, x_scales, x_cols[c - 1], E4M3_X4)
        quantise(nc, x_grouped[N_TILES - 1], x_codes, x_scales, x_cols[N_TILES - 1], E4M3_X4)

        g_cols = [slice(t * N_TILE, (t + 1) * N_TILE) for t in range(CHUNKS)]
        g_by_row = g_raw[:].rearrange("p j (m e) -> p m j e", e=ROWS)
        g_grouped = []
        for t in range(CHUNKS):
            gg = stage.tile([P, N_TILE * PACK], BF16, align_bytes=64, name="grouped")
            dst = gg[:].rearrange("p (e m j) -> p m j e", e=CHUNK_ROWS, j=PACK)
            src = g_by_row[:, :, :, t * CHUNK_ROWS : (t + 1) * CHUNK_ROWS]
            if t == 0:
                nc.vector.tensor_copy(out=dst, in_=src)
            else:
                nc.scalar.copy(out=dst, in_=src)
            g_grouped.append(gg)
        quantise(nc, g_grouped[0], g_codes, g_scales, g_cols[0], E5M2_X4)

        e = 0
        for rows in STORES:
            result = results.tile([P, RESULT_ROWS, IN_F], F32)
            for r in range(rows):
                if e % CHUNK_ROWS == 0 and e // CHUNK_ROWS + 1 < CHUNKS:
                    t = e // CHUNK_ROWS + 1
                    quantise(nc, g_grouped[t], g_codes, g_scales, g_cols[t], E5M2_X4)
                mask_t, mask_r = mask_of_row[e]
                m_cols = slice(e * P, (e + 1) * P)
                for n_cols in x_cols:
                    acc = psum.tile([P, N_TILE], F32)
                    nc.tensor.matmul_mx(
                        out=acc[:],
                        lhsT=g_codes[:, m_cols].bitcast(E5M2_X4),
                        lhsT_scale=g_scales[:, m_cols],
                        rhs=x_codes[:, n_cols].bitcast(E4M3_X4),
                        rhs_scale=x_scales[:, n_cols],
                        start=True,
                        stop=True,
                    )
                    nc.vector.tensor_tensor(
                        out=result[:, r, n_cols],
                        in0=acc[:],
                        in1=mask_t[:, mask_r, n_cols],
                        op=mybir.AluOpType.mult,
                    )
                e += 1
            nc.sync.dma_start(out=out_rows[:, e - rows : e, :], in_=result[:, :rows, :])
